import numpy as np
import ml_dtypes


def mxq(x, axis, fmt="e4m3"):
    dtype, down = {"e4m3": (ml_dtypes.float8_e4m3fn, 7), "e5m2": (ml_dtypes.float8_e5m2, 14)}[fmt]
    v = np.moveaxis(np.asarray(x, np.float32).astype(ml_dtypes.bfloat16).astype(np.float64), axis, -1)
    blocks = v.reshape(v.shape[:-1] + (-1, 32))
    amax = np.abs(blocks).max(-1, keepdims=True)
    byte = np.maximum(np.where(amax > 0, np.frexp(amax)[1] - 1 + 127, 0) - down, 1)
    scale = np.exp2(byte - 127.0)
    codes = (blocks / scale).astype(np.float32).astype(dtype).astype(np.float64)
    return np.moveaxis((codes * scale).reshape(v.shape), -1, axis)


WIDE = False


def mx_kscale(k):
    if not WIDE:
        return np.ones(k)
    levels = np.array([10, -10, 5, -5, 0])
    a = np.random.permutation(np.resize(levels, k // 512 * 4)).reshape(k // 512, 4)
    idx = np.arange(k)
    return np.exp2(a[idx // 512, idx % 128 // 32])


BF16 = ml_dtypes.bfloat16


def bf(x):
    return np.asarray(x, np.float32).astype(BF16)


def f64(x):
    return np.asarray(x).astype(np.float64)


N_EMBD = 512
N_EXP = 4
DIM_HIDDEN = 2048
B = 2
CAP = 128


def erf(z):
    a = np.clip(z, -6.0, 6.0)
    a2 = 2.0 * a * a
    term = a.copy()
    tot = a.copy()
    for n in range(1, 120):
        term = term * a2 / (2 * n + 1)
        tot = tot + term
    return 2.0 / np.sqrt(np.pi) * np.exp(-a * a) * tot


def gelu_exact(v):
    return 0.5 * v * (1.0 + erf(v / np.sqrt(2.0)))


def setup_inputs():
    s = mx_kscale(N_EMBD)
    t = mx_kscale(DIM_HIDDEN)
    col = np.concatenate([t, np.ones(DIM_HIDDEN)])
    return {"x": bf(np.random.standard_normal((B, N_EXP, CAP, N_EMBD))),
            "c_fc": bf(np.random.uniform(-0.08, 0.08, (N_EXP, N_EMBD, 2 * DIM_HIDDEN)) / s[None, :, None] * col),
            "c_proj": bf(np.random.uniform(-0.06, 0.06, (N_EXP, DIM_HIDDEN, N_EMBD)) / t[None, :, None]),
            "gamma": bf((1.0 + 0.1 * np.random.standard_normal(N_EMBD)) * s),
            "mult_bias": bf(1.0 + 0.1 * np.random.standard_normal(DIM_HIDDEN))}


def reference(x, c_fc, c_proj, gamma, mult_bias):
    h = np.transpose(f64(x), (1, 0, 2, 3))
    scale = N_EMBD ** 0.5
    l2 = np.sqrt(np.sum(h * h, axis=-1, keepdims=True))
    h = h / np.maximum(l2, 1e-12) * f64(gamma) * scale
    u = mxq(h, 3, "e4m3") @ mxq(f64(c_fc), 1, "e4m3")[:, None]
    v, gate = u[..., :DIM_HIDDEN], u[..., DIM_HIDDEN:]
    g = gelu_exact(gate) * v * f64(mult_bias)
    out = mxq(g, 3, "e4m3") @ mxq(f64(c_proj), 1, "e4m3")[:, None]
    return np.transpose(out, (1, 0, 2, 3))

@@ -1,0 +1,296 @@
+from contextlib import ExitStack
+
+import concourse.mybir as mybir
+from concourse.masks import make_identity
+
+BF16 = mybir.dt.bfloat16
+F32 = mybir.dt.float32
+U32 = mybir.dt.uint32
+U8 = mybir.dt.uint8
+FP8X4 = mybir.dt.float8_e4m3fn_x4
+ACT = mybir.ActivationFunctionType
+ALU = mybir.AluOpType
+
+P = 128
+D = 512
+H = 2048
+NE = 4
+NB = 2
+TOK = NB * P
+UNITS = NE * 4
+
+FLOPS = 2 * NE * TOK * (D * 2 * H + H * D)
+
+MANUAL = False
+RAW_BUFS = 4
+VFC_DEFAULT = 112
+VFC = {0: 1024}
+
+
+def regroup(copy, dst, src, c0, c1):
+    copy(
+        out=dst[:, c0:c1, :].rearrange("p (c i) t -> p c t i", i=4),
+        in_=src[:, :, c0:c1].rearrange("p t (c i) -> p c t i", i=4),
+    )
+
+
+def tile_mlp_kernel(tc, x, c_fc, c_proj, gamma, mult_bias, out):
+    nc = tc.nc
+    with ExitStack() as ctx:
+        if MANUAL:
+            ctx.enter_context(tc.manual_schedule())
+        const = ctx.enter_context(tc.tile_pool(name="const", bufs=1))
+        rawp = ctx.enter_context(tc.tile_pool(name="raw", bufs=RAW_BUFS))
+        grpp = ctx.enter_context(tc.tile_pool(name="grp", bufs=3))
+        codp = ctx.enter_context(tc.tile_pool(name="cod", bufs=4))
+        actp = ctx.enter_context(tc.tile_pool(name="act", bufs=4))
+        gp = ctx.enter_context(tc.tile_pool(name="g", bufs=2))
+        outp = ctx.enter_context(tc.tile_pool(name="outp", bufs=4))
+        ps = ctx.enter_context(tc.psum_pool(name="ps", bufs=6))
+        pso = ctx.enter_context(tc.psum_pool(name="pso", bufs=1))
+
+        raw = {}
+        cod = {}
+        grp = {}
+        bank = {}
+        gel = {}
+        pla = {}
+        gq = {}
+        acc = {}
+
+        def load_fc(u, half):
+            e, g = divmod(u, 4)
+            if half == 0:
+                raw_fc = rawp.tile([P, 4, 1024], BF16, name="raw_fc")
+                raw[("fc", u)] = raw_fc
+            col = half * H + 512 * g
+            nc.sync.dma_start(
+                out=raw[("fc", u)][:, :, 512 * half : 512 * half + 512],
+                in_=c_fc[e].rearrange("(t p) n -> p t n", p=P)[:, :, col : col + 512],
+            )
+
+        def load_pj(u):
+            e, g = divmod(u, 4)
+            raw_pj = rawp.tile([P, 4, 512], BF16, name="raw_pj")
+            raw[("pj", u)] = raw_pj
+            nc.sync.dma_start(
+                out=raw_pj,
+                in_=c_proj[e, 512 * g : 512 * g + 512, :].rearrange("(t p) n -> p t n", p=P),
+            )
+
+        def load(u):
+            load_fc(u, 0)
+            load_fc(u, 1)
+            load_pj(u)
+
+        g_row = const.tile([P, D], BF16, name="g_row")
+        nc.vector.memset(g_row, 0.0)
+        nc.scalar.dma_start(out=g_row[0:1, :], in_=gamma.rearrange("(o d) -> o d", o=1))
+        mb_rows = const.tile([P, P], BF16, name="mb_rows")
+        nc.vector.memset(mb_rows, 0.0)
+        nc.scalar.dma_start(out=mb_rows[0:16, :], in_=mult_bias.rearrange("(c p) -> c p", p=P))
+        ones = const.tile([P, P], BF16, name="ones")
+        nc.vector.memset(ones, 1.0)
+        warm = const.tile([P, 1], F32, name="warm")
+        nc.vector.memset(warm, 1.0)
+        warm2 = const.tile([P, 1], F32, name="warm2")
+        nc.scalar.activation(out=warm2, in_=warm, func=ACT.Sqrt)
+        ident = const.tile([P, P], BF16, name="ident")
+        make_identity(nc, ident)
+
+        x_sb = const.tile([P, 8, D], BF16, name="x_sb")
+        load_fc(0, 0)
+        nc.sync.dma_start(out=x_sb[:, 0:4, :], in_=x[0].rearrange("e n d -> n e d"))
+        load_fc(0, 1)
+        nc.sync.dma_start(out=x_sb[:, 4:8, :], in_=x[1].rearrange("e n d -> n e d"))
+        load_pj(0)
+        for u in range(1, RAW_BUFS):
+            load(u)
+
+        def w_copy(u):
+            vfc = VFC.get(u, VFC_DEFAULT)
+            grp_fc = grpp.tile([P, 1024, 4], BF16, name="grp_fc", align_bytes=64)
+            grp_pj = grpp.tile([P, 512, 4], BF16, name="grp_pj", align_bytes=64)
+            grp[("fc", u)] = grp_fc
+            grp[("pj", u)] = grp_pj
+            if vfc < 1024:
+                regroup(nc.scalar.copy, grp_fc, raw[("fc", u)], vfc, 1024)
+            if vfc > 512:
+                regroup(nc.vector.tensor_copy, grp_fc, raw[("fc", u)], 0, 512)
+                regroup(nc.vector.tensor_copy, grp_fc, raw[("fc", u)], 512, vfc)
+            elif vfc > 0:
+                regroup(nc.vector.tensor_copy, grp_fc, raw[("fc", u)], 0, vfc)
+            regroup(nc.vector.tensor_copy, grp_pj, raw[("pj", u)], 0, 512)
+
+        def w_quant(u, which):
+            width = 1024 if which == "fc" else 512
+            codes = codp.tile([P, width], U32, name="cod_" + which, align_bytes=64)
+            scales = codp.tile([P, width], U8, name="scl_" + which, align_bytes=64)
+            cod[(which, u)] = (codes, scales)
+            nc.vector.quantize_mx(
+                out=codes.bitcast(FP8X4),
+                scales=scales,
+                in_=grp[(which, u)].rearrange("p w j -> p (w j)"),
+            )
+
+        def mm1(u):
+            e = u // 4
+            codes, scales = cod[("fc", u)]
+            for kind in ("g", "v"):
+                base = 512 if kind == "g" else 0
+                for j in range(2):
+                    pt = ps.tile([P, 2, TOK], F32, tag="u", name="p" + kind)
+                    bank[(kind, u, j)] = pt
+                    for s in range(2):
+                        c0 = base + 128 * (2 * j + s)
+                        nc.tensor.matmul_mx(
+                            out=pt[:, s, :],
+                            lhsT=codes[:, c0 : c0 + 128].bitcast(FP8X4),
+                            lhsT_scale=scales[:, c0 : c0 + 128],
+                            rhs=hq_c[:, e, :].bitcast(FP8X4),
+                            rhs_scale=hq_s[:, e, :],
+                            start=True,
+                            stop=True,
+                        )
+
+        def g_gelu(u):
+            for j in range(2):
+                a = actp.tile([P, 2, TOK], F32, name="gelu")
+                gel[(u, j)] = a
+                nc.scalar.activation(out=a, in_=bank[("g", u, j)], func=ACT.Gelu)
+
+        def g_mul(u):
+            g = u % 4
+            planes = gp.tile([P, 4, TOK], BF16, name="planes")
+            pla[u] = planes
+            for c in range(4):
+                nc.vector.scalar_tensor_tensor(
+                    out=planes[:, c, :],
+                    in0=bank[("v", u, c // 2)][:, c % 2, :],
+                    scalar=mbT[:, 4 * g + c : 4 * g + c + 1],
+                    in1=gel[(u, c // 2)][:, c % 2, :],
+                    op0=ALU.mult,
+                    op1=ALU.mult,
+                )
+
+        def g_regroup(u):
+            gg = gp.tile([P, TOK, 4], BF16, name="gg", align_bytes=64)
+            grp[("g", u)] = gg
+            regroup(nc.vector.tensor_copy, gg, pla[u], 0, TOK)
+
+        def g_quant(u):
+            codes = gp.tile([P, TOK], U32, name="gq_c", align_bytes=64)
+            scales = gp.tile([P, TOK], U8, name="gq_s", align_bytes=64)
+            gq[u] = (codes, scales)
+            nc.vector.quantize_mx(
+                out=codes.bitcast(FP8X4),
+                scales=scales,
+                in_=grp[("g", u)].rearrange("p w j -> p (w j)"),
+            )
+
+        def mm2(u):
+            e, g = divmod(u, 4)
+            if g == 0:
+                for b in range(NB):
+                    acc[(e, b)] = pso.tile([P, D], F32, tag="po%d" % b, name="po%d" % b)
+            codes, scales = gq[u]
+            wc, ws = cod[("pj", u)]
+            for b in range(NB):
+                nc.tensor.matmul_mx(
+                    out=acc[(e, b)],
+                    lhsT=codes[:, P * b : P * b + P].bitcast(FP8X4),
+                    lhsT_scale=scales[:, P * b : P * b + P],
+                    rhs=wc.bitcast(FP8X4),
+                    rhs_scale=ws,
+                    start=(g == 0),
+                    stop=(g == 3),
+                )
+
+        def store(e):
+            for b in range(NB):
+                osb = outp.tile([P, D], F32, name="osb")
+                nc.scalar.copy(out=osb, in_=acc[(e, b)])
+                nc.sync.dma_start(out=out[b, e], in_=osb)
+
+        w_copy(0)
+        load(RAW_BUFS)
+
+        ss = const.tile([P, 8], F32, name="ss")
+        junk = const.tile([P, D], BF16, name="junk")
+        for i in range(8):
+            nc.scalar.activation(
+                out=junk, in_=x_sb[:, i, :], func=ACT.Square, accum_out=ss[:, i : i + 1]
+            )
+        ssc = const.tile([P, 8], F32, name="ssc")
+        nc.vector.tensor_scalar(
+            out=ssc, in0=ss, scalar1=1e-24, scalar2=1.0 / D, op0=ALU.max, op1=ALU.mult
+        )
+        l2 = const.tile([P, 8], F32, name="l2")
+        nc.scalar.activation(out=l2, in_=ssc, func=ACT.Sqrt)
+        rn = const.tile([P, 8], F32, name="rn")
+        nc.vector.reciprocal(out=rn, in_=l2)
+
+        gps = ps.tile([P, D], F32, tag="u", name="gps")
+        nc.tensor.matmul(out=gps, lhsT=ones, rhs=g_row, start=True, stop=True)
+        pm = ps.tile([P, P], BF16, tag="u", name="pm")
+        nc.tensor.transpose(pm, mb_rows, ident)
+        mbT = const.tile([P, 16], F32, name="mbT")
+        nc.vector.tensor_copy(out=mbT, in_=pm[:, 0:16])
+
+        h_sb = const.tile([P, 8, D], BF16, name="h_sb")
+        hq_c = const.tile([P, NE, TOK], U32, name="hq_c", align_bytes=64)
+        hq_s = const.tile([P, NE, TOK], U8, name="hq_s", align_bytes=64)
+        for e in range(NE):
+            for b in range(NB):
+                i = 4 * b + e
+                nc.vector.scalar_tensor_tensor(
+                    out=h_sb[:, i, :],
+                    in0=x_sb[:, i, :],
+                    scalar=rn[:, i : i + 1],
+                    in1=gps,
+                    op0=ALU.mult,
+                    op1=ALU.mult,
+                )
+            pT = ps.tile([P, NB, 4, P], BF16, tag="u", name="pT")
+            for b in range(NB):
+                for t in range(4):
+                    nc.tensor.transpose(
+                        pT[:, b, t, :], h_sb[:, 4 * b + e, P * t : P * t + P], ident
+                    )
+            hg = gp.tile([P, NB, P, 4], BF16, name="hg", align_bytes=64)
+            nc.scalar.copy(out=hg, in_=pT.rearrange("p b t r -> p b r t"))
+            nc.vector.quantize_mx(
+                out=hq_c[:, e, :].bitcast(FP8X4),
+                scales=hq_s[:, e, :],
+                in_=hg.rearrange("p b r t -> p (b r t)"),
+            )
+            if e == 0:
+                w_copy(1)
+                load(RAW_BUFS + 1)
+
+        for k in range(-1, UNITS):
+            if k + 1 < UNITS:
+                w_quant(k + 1, "fc")
+            if k >= 1:
+                g_quant(k - 1)
+            if k + 1 < UNITS:
+                w_quant(k + 1, "pj")
+            if k >= 1:
+                mm2(k - 1)
+            if k >= 0:
+                g_gelu(k)
+            if k + 1 < UNITS:
+                mm1(k + 1)
+            if k >= 0:
+                g_mul(k)
+            if k >= 0 and k + 2 < UNITS:
+                w_copy(k + 2)
+                if k + 2 + RAW_BUFS < UNITS:
+                    load(k + 2 + RAW_BUFS)
+            if k >= 1 and (k - 1) % 4 == 3:
+                store((k - 1) // 4)
+            if k >= 0:
+                g_regroup(k)
+        g_quant(UNITS - 1)
+        mm2(UNITS - 1)
+        store(NE - 1)

@@ -21,10 +21,10 @@ UNITS = NE * 4
 
 FLOPS = 2 * NE * TOK * (D * 2 * H + H * D)
 
-MANUAL = False
+MANUAL = True
 RAW_BUFS = 4
-VFC_DEFAULT = 112
-VFC = {0: 1024}
+SHARE_DEFAULT = (112, 512)
+SHARE = {0: (1024, 0), 1: (512, 512)}
 
 
 def regroup(copy, dst, src, c0, c1):
@@ -46,6 +46,7 @@ def tile_mlp_kernel(tc, x, c_fc, c_proj, gamma, mult_bias, out):
         actp = ctx.enter_context(tc.tile_pool(name="act", bufs=4))
         gp = ctx.enter_context(tc.tile_pool(name="g", bufs=2))
         outp = ctx.enter_context(tc.tile_pool(name="outp", bufs=4))
+        hgp = ctx.enter_context(tc.tile_pool(name="hgp", bufs=4))
         ps = ctx.enter_context(tc.psum_pool(name="ps", bufs=6))
         pso = ctx.enter_context(tc.psum_pool(name="pso", bufs=1))
 
@@ -57,12 +58,12 @@ def tile_mlp_kernel(tc, x, c_fc, c_proj, gamma, mult_bias, out):
         pla = {}
         gq = {}
         acc = {}
+        hgs = {}
 
         def load_fc(u, half):
             e, g = divmod(u, 4)
             if half == 0:
-                raw_fc = rawp.tile([P, 4, 1024], BF16, name="raw_fc")
-                raw[("fc", u)] = raw_fc
+                raw[("fc", u)] = rawp.tile([P, 4, 1024], BF16, name="raw_fc")
             col = half * H + 512 * g
             nc.sync.dma_start(
                 out=raw[("fc", u)][:, :, 512 * half : 512 * half + 512],
@@ -71,56 +72,43 @@ def tile_mlp_kernel(tc, x, c_fc, c_proj, gamma, mult_bias, out):
 
         def load_pj(u):
             e, g = divmod(u, 4)
-            raw_pj = rawp.tile([P, 4, 512], BF16, name="raw_pj")
-            raw[("pj", u)] = raw_pj
+            raw[("pj", u)] = rawp.tile([P, 4, 512], BF16, name="raw_pj")
             nc.sync.dma_start(
-                out=raw_pj,
+                out=raw[("pj", u)],
                 in_=c_proj[e, 512 * g : 512 * g + 512, :].rearrange("(t p) n -> p t n", p=P),
             )
 
         def load(u):
-            load_fc(u, 0)
-            load_fc(u, 1)
-            load_pj(u)
+            if u < UNITS:
+                load_fc(u, 0)
+                load_fc(u, 1)
+                load_pj(u)
 
-        g_row = const.tile([P, D], BF16, name="g_row")
-        nc.vector.memset(g_row, 0.0)
-        nc.scalar.dma_start(out=g_row[0:1, :], in_=gamma.rearrange("(o d) -> o d", o=1))
-        mb_rows = const.tile([P, P], BF16, name="mb_rows")
-        nc.vector.memset(mb_rows, 0.0)
-        nc.scalar.dma_start(out=mb_rows[0:16, :], in_=mult_bias.rearrange("(c p) -> c p", p=P))
-        ones = const.tile([P, P], BF16, name="ones")
-        nc.vector.memset(ones, 1.0)
-        warm = const.tile([P, 1], F32, name="warm")
-        nc.vector.memset(warm, 1.0)
-        warm2 = const.tile([P, 1], F32, name="warm2")
-        nc.scalar.activation(out=warm2, in_=warm, func=ACT.Sqrt)
-        ident = const.tile([P, P], BF16, name="ident")
-        make_identity(nc, ident)
+        def w_alloc(u):
+            grp[("fc", u)] = grpp.tile([P, 1024, 4], BF16, name="grp_fc", align_bytes=64)
+            grp[("pj", u)] = grpp.tile([P, 512, 4], BF16, name="grp_pj", align_bytes=64)
 
-        x_sb = const.tile([P, 8, D], BF16, name="x_sb")
-        load_fc(0, 0)
-        nc.sync.dma_start(out=x_sb[:, 0:4, :], in_=x[0].rearrange("e n d -> n e d"))
-        load_fc(0, 1)
-        nc.sync.dma_start(out=x_sb[:, 4:8, :], in_=x[1].rearrange("e n d -> n e d"))
-        load_pj(0)
-        for u in range(1, RAW_BUFS):
-            load(u)
+        def w_copy_s(u):
+            vfc, vpj = SHARE.get(u, SHARE_DEFAULT)
+            if vfc < 1024:
+                regroup(nc.scalar.copy, grp[("fc", u)], raw[("fc", u)], vfc, 1024)
+            if vpj < 512:
+                regroup(nc.scalar.copy, grp[("pj", u)], raw[("pj", u)], vpj, 512)
+
+        def w_copy_v(u):
+            vfc, vpj = SHARE.get(u, SHARE_DEFAULT)
+            if vfc > 512:
+                regroup(nc.vector.tensor_copy, grp[("fc", u)], raw[("fc", u)], 0, 512)
+                regroup(nc.vector.tensor_copy, grp[("fc", u)], raw[("fc", u)], 512, vfc)
+            elif vfc > 0:
+                regroup(nc.vector.tensor_copy, grp[("fc", u)], raw[("fc", u)], 0, vfc)
+            if vpj > 0:
+                regroup(nc.vector.tensor_copy, grp[("pj", u)], raw[("pj", u)], 0, vpj)
 
         def w_copy(u):
-            vfc = VFC.get(u, VFC_DEFAULT)
-            grp_fc = grpp.tile([P, 1024, 4], BF16, name="grp_fc", align_bytes=64)
-            grp_pj = grpp.tile([P, 512, 4], BF16, name="grp_pj", align_bytes=64)
-            grp[("fc", u)] = grp_fc
-            grp[("pj", u)] = grp_pj
-            if vfc < 1024:
-                regroup(nc.scalar.copy, grp_fc, raw[("fc", u)], vfc, 1024)
-            if vfc > 512:
-                regroup(nc.vector.tensor_copy, grp_fc, raw[("fc", u)], 0, 512)
-                regroup(nc.vector.tensor_copy, grp_fc, raw[("fc", u)], 512, vfc)
-            elif vfc > 0:
-                regroup(nc.vector.tensor_copy, grp_fc, raw[("fc", u)], 0, vfc)
-            regroup(nc.vector.tensor_copy, grp_pj, raw[("pj", u)], 0, 512)
+            w_alloc(u)
+            w_copy_s(u)
+            w_copy_v(u)
 
         def w_quant(u, which):
             width = 1024 if which == "fc" else 512
@@ -206,14 +194,42 @@ def tile_mlp_kernel(tc, x, c_fc, c_proj, gamma, mult_bias, out):
                     stop=(g == 3),
                 )
 
-        def store(e):
+        def store(e, copies):
             for b in range(NB):
                 osb = outp.tile([P, D], F32, name="osb")
-                nc.scalar.copy(out=osb, in_=acc[(e, b)])
+                copies[b](out=osb, in_=acc[(e, b)])
                 nc.sync.dma_start(out=out[b, e], in_=osb)
 
-        w_copy(0)
-        load(RAW_BUFS)
+        def h_quant(e):
+            nc.vector.quantize_mx(
+                out=hq_c[:, e, :].bitcast(FP8X4),
+                scales=hq_s[:, e, :],
+                in_=hgs[e].rearrange("p b r t -> p (b r t)"),
+            )
+
+        g_row = const.tile([P, D], BF16, name="g_row")
+        nc.vector.memset(g_row, 0.0)
+        nc.scalar.dma_start(out=g_row[0:1, :], in_=gamma.rearrange("(o d) -> o d", o=1))
+        mb_rows = const.tile([P, P], BF16, name="mb_rows")
+        nc.vector.memset(mb_rows, 0.0)
+        nc.scalar.dma_start(out=mb_rows[0:16, :], in_=mult_bias.rearrange("(c p) -> c p", p=P))
+        ones = const.tile([P, P], BF16, name="ones")
+        nc.vector.memset(ones, 1.0)
+        warm = const.tile([P, 1], F32, name="warm")
+        nc.vector.memset(warm, 1.0)
+        warm2 = const.tile([P, 1], F32, name="warm2")
+        nc.scalar.activation(out=warm2, in_=warm, func=ACT.Sqrt)
+        ident = const.tile([P, P], BF16, name="ident")
+        make_identity(nc, ident)
+
+        x_sb = const.tile([P, 8, D], BF16, name="x_sb")
+        nc.sync.dma_start(out=x_sb[:, 0:4, :], in_=x[0].rearrange("e n d -> n e d"))
+        load_fc(0, 0)
+        load_fc(0, 1)
+        nc.sync.dma_start(out=x_sb[:, 4:8, :], in_=x[1].rearrange("e n d -> n e d"))
+        load_pj(0)
+        for u in range(1, RAW_BUFS):
+            load(u)
 
         ss = const.tile([P, 8], F32, name="ss")
         junk = const.tile([P, D], BF16, name="junk")
@@ -221,6 +237,8 @@ def tile_mlp_kernel(tc, x, c_fc, c_proj, gamma, mult_bias, out):
             nc.scalar.activation(
                 out=junk, in_=x_sb[:, i, :], func=ACT.Square, accum_out=ss[:, i : i + 1]
             )
+        w_alloc(0)
+        w_copy_v(0)
         ssc = const.tile([P, 8], F32, name="ssc")
         nc.vector.tensor_scalar(
             out=ssc, in0=ss, scalar1=1e-24, scalar2=1.0 / D, op0=ALU.max, op1=ALU.mult
@@ -229,6 +247,10 @@ def tile_mlp_kernel(tc, x, c_fc, c_proj, gamma, mult_bias, out):
         nc.scalar.activation(out=l2, in_=ssc, func=ACT.Sqrt)
         rn = const.tile([P, 8], F32, name="rn")
         nc.vector.reciprocal(out=rn, in_=l2)
+        warm3 = const.tile([P, 1], F32, name="warm3")
+        nc.scalar.activation(out=warm3, in_=warm, func=ACT.Gelu)
+        w_copy_s(0)
+        load(RAW_BUFS)
 
         gps = ps.tile([P, D], F32, tag="u", name="gps")
         nc.tensor.matmul(out=gps, lhsT=ones, rhs=g_row, start=True, stop=True)
@@ -257,40 +279,38 @@ def tile_mlp_kernel(tc, x, c_fc, c_proj, gamma, mult_bias, out):
                     nc.tensor.transpose(
                         pT[:, b, t, :], h_sb[:, 4 * b + e, P * t : P * t + P], ident
                     )
-            hg = gp.tile([P, NB, P, 4], BF16, name="hg", align_bytes=64)
-            nc.scalar.copy(out=hg, in_=pT.rearrange("p b t r -> p b r t"))
-            nc.vector.quantize_mx(
-                out=hq_c[:, e, :].bitcast(FP8X4),
-                scales=hq_s[:, e, :],
-                in_=hg.rearrange("p b r t -> p (b r t)"),
-            )
-            if e == 0:
-                w_copy(1)
-                load(RAW_BUFS + 1)
+            hgs[e] = hgp.tile([P, NB, P, 4], BF16, name="hg", align_bytes=64)
+            nc.scalar.copy(out=hgs[e], in_=pT.rearrange("p b t r -> p b r t"))
 
-        for k in range(-1, UNITS):
+        w_quant(0, "fc")
+        h_quant(0)
+        w_quant(0, "pj")
+        mm1(0)
+        w_copy(1)
+        load(RAW_BUFS + 1)
+        h_quant(1)
+
+        for k in range(UNITS):
             if k + 1 < UNITS:
                 w_quant(k + 1, "fc")
             if k >= 1:
                 g_quant(k - 1)
+            if k < 2:
+                h_quant(k + 2)
             if k + 1 < UNITS:
                 w_quant(k + 1, "pj")
             if k >= 1:
                 mm2(k - 1)
-            if k >= 0:
-                g_gelu(k)
+            g_gelu(k)
             if k + 1 < UNITS:
                 mm1(k + 1)
-            if k >= 0:
-                g_mul(k)
-            if k >= 0 and k + 2 < UNITS:
+            g_mul(k)
+            if k + 2 < UNITS:
                 w_copy(k + 2)
-                if k + 2 + RAW_BUFS < UNITS:
-                    load(k + 2 + RAW_BUFS)
+                load(k + 2 + RAW_BUFS)
             if k >= 1 and (k - 1) % 4 == 3:
-                store((k - 1) // 4)
-            if k >= 0:
-                g_regroup(k)
+                store((k - 1) // 4, (nc.scalar.copy, nc.scalar.copy))
+            g_regroup(k)
         g_quant(UNITS - 1)
         mm2(UNITS - 1)
-        store(NE - 1)
+        store(NE - 1, (nc.scalar.copy, nc.vector.tensor_copy))

@@ -23,7 +23,7 @@ FLOPS = 2 * NE * TOK * (D * 2 * H + H * D)
 
 MANUAL = True
 RAW_BUFS = 4
-SHARE_DEFAULT = (112, 512)
+SHARE_DEFAULT = (304, 512)
 SHARE = {0: (1024, 0), 1: (512, 512)}
 
 
@@ -149,14 +149,14 @@ def tile_mlp_kernel(tc, x, c_fc, c_proj, gamma, mult_bias, out):
 
         def g_mul(u):
             g = u % 4
-            planes = gp.tile([P, 4, TOK], BF16, name="planes")
+            planes = gp.tile([P, TOK // 8, 4, 8], BF16, name="planes")
             pla[u] = planes
             for c in range(4):
                 nc.vector.scalar_tensor_tensor(
-                    out=planes[:, c, :],
-                    in0=bank[("v", u, c // 2)][:, c % 2, :],
+                    out=planes[:, :, c, :],
+                    in0=bank[("v", u, c // 2)][:, c % 2, :].rearrange("p (a b) -> p a b", b=8),
                     scalar=mbT[:, 4 * g + c : 4 * g + c + 1],
-                    in1=gel[(u, c // 2)][:, c % 2, :],
+                    in1=gel[(u, c // 2)][:, c % 2, :].rearrange("p (a b) -> p a b", b=8),
                     op0=ALU.mult,
                     op1=ALU.mult,
                 )
@@ -164,7 +164,27 @@ def tile_mlp_kernel(tc, x, c_fc, c_proj, gamma, mult_bias, out):
         def g_regroup(u):
             gg = gp.tile([P, TOK, 4], BF16, name="gg", align_bytes=64)
             grp[("g", u)] = gg
-            regroup(nc.vector.tensor_copy, gg, pla[u], 0, TOK)
+            nc.vector.tensor_copy(
+                out=gg.rearrange("p (a b) t -> p a b t", b=8),
+                in_=pla[u].rearrange("p a t b -> p a b t"),
+            )
+
+        def g_inter(u):
+            pb = ps.tile([P, TOK, 4], BF16, tag="u", name="pb")
+            bank[("b", u)] = pb
+            for j in range(NB):
+                nc.tensor.matmul(
+                    out=pb[:, P * j : P * j + P, :].rearrange("p r t -> p (r t)"),
+                    lhsT=ident,
+                    rhs=pla[u][:, 16 * j : 16 * j + 16, :, :].rearrange("p a t b -> p a b t"),
+                    start=True,
+                    stop=True,
+                )
+
+        def g_copy(u):
+            gg = gp.tile([P, TOK, 4], BF16, name="gg", align_bytes=64)
+            grp[("g", u)] = gg
+            nc.scalar.copy(out=gg, in_=bank[("b", u)])
 
         def g_quant(u):
             codes = gp.tile([P, TOK], U32, name="gq_c", align_bytes=64)
@@ -293,24 +313,27 @@ def tile_mlp_kernel(tc, x, c_fc, c_proj, gamma, mult_bias, out):
         for k in range(UNITS):
             if k + 1 < UNITS:
                 w_quant(k + 1, "fc")
-            if k >= 1:
-                g_quant(k - 1)
             if k < 2:
                 h_quant(k + 2)
             if k + 1 < UNITS:
                 w_quant(k + 1, "pj")
-            if k >= 1:
-                mm2(k - 1)
             g_gelu(k)
+            if k >= 1:
+                g_copy(k - 1)
             if k + 1 < UNITS:
                 mm1(k + 1)
             g_mul(k)
+            if k + 1 < UNITS:
+                g_inter(k)
+            if k >= 1:
+                g_quant(k - 1)
+                mm2(k - 1)
             if k + 2 < UNITS:
                 w_copy(k + 2)
                 load(k + 2 + RAW_BUFS)
             if k >= 1 and (k - 1) % 4 == 3:
                 store((k - 1) // 4, (nc.scalar.copy, nc.scalar.copy))
-            g_regroup(k)
+        g_regroup(UNITS - 1)
         g_quant(UNITS - 1)
         mm2(UNITS - 1)
         store(NE - 1, (nc.scalar.copy, nc.vector.tensor_copy))

@@ -23,7 +23,7 @@ FLOPS = 2 * NE * TOK * (D * 2 * H + H * D)
 
 MANUAL = True
 RAW_BUFS = 4
-SHARE_DEFAULT = (304, 512)
+SHARE_DEFAULT = (432, 512)
 SHARE = {0: (1024, 0), 1: (512, 512)}
 
 

@@ -23,14 +23,14 @@ FLOPS = 2 * NE * TOK * (D * 2 * H + H * D)
 
 MANUAL = True
 RAW_BUFS = 4
-SHARE_DEFAULT = (432, 512)
+SHARE_DEFAULT = (304, 512)
 SHARE = {0: (1024, 0), 1: (512, 512)}
 
 
-def regroup(copy, dst, src, c0, c1):
+def regroup(copy, dst, c0, c1, src, s0):
     copy(
         out=dst[:, c0:c1, :].rearrange("p (c i) t -> p c t i", i=4),
-        in_=src[:, :, c0:c1].rearrange("p t (c i) -> p c t i", i=4),
+        in_=src[:, :, s0 : s0 + c1 - c0].rearrange("p t (c i) -> p c t i", i=4),
     )
 
 
@@ -41,6 +41,7 @@ def tile_mlp_kernel(tc, x, c_fc, c_proj, gamma, mult_bias, out):
             ctx.enter_context(tc.manual_schedule())
         const = ctx.enter_context(tc.tile_pool(name="const", bufs=1))
         rawp = ctx.enter_context(tc.tile_pool(name="raw", bufs=RAW_BUFS))
+        rawf = ctx.enter_context(tc.tile_pool(name="rawf", bufs=2))
         grpp = ctx.enter_context(tc.tile_pool(name="grp", bufs=3))
         codp = ctx.enter_context(tc.tile_pool(name="cod", bufs=4))
         actp = ctx.enter_context(tc.tile_pool(name="act", bufs=4))
@@ -62,13 +63,16 @@ def tile_mlp_kernel(tc, x, c_fc, c_proj, gamma, mult_bias, out):
 
         def load_fc(u, half):
             e, g = divmod(u, 4)
-            if half == 0:
-                raw[("fc", u)] = rawp.tile([P, 4, 1024], BF16, name="raw_fc")
             col = half * H + 512 * g
             nc.sync.dma_start(
-                out=raw[("fc", u)][:, :, 512 * half : 512 * half + 512],
+                out=raw[("fc", e)][:, :, col : col + 512],
                 in_=c_fc[e].rearrange("(t p) n -> p t n", p=P)[:, :, col : col + 512],
             )
+
+        def load_fc_rows(e):
+            raw[("fc", e)] = rawf.tile([P, 4, 2 * H], BF16, name="raw_fc")
+            for t in range(4):
+                nc.sync.dma_start(out=raw[("fc", e)][:, t, :], in_=c_fc[e, P * t : P * t + P, :])
 
         def load_pj(u):
             e, g = divmod(u, 4)
@@ -79,10 +83,23 @@ def tile_mlp_kernel(tc, x, c_fc, c_proj, gamma, mult_bias, out):
             )
 
         def load(u):
-            if u < UNITS:
-                load_fc(u, 0)
-                load_fc(u, 1)
-                load_pj(u)
+            load_fc(u, 0)
+            load_fc(u, 1)
+            load_pj(u)
+
+        def refill(u):
+            if u + RAW_BUFS < UNITS:
+                load_pj(u + RAW_BUFS)
+            if u % 4 == 3 and u // 4 + 2 < NE:
+                load_fc_rows(u // 4 + 2)
+
+        def fc_copy(copy, u, c0, c1):
+            e, g = divmod(u, 4)
+            for half in range(2):
+                a = max(c0, 512 * half)
+                b = min(c1, 512 * half + 512)
+                if a < b:
+                    regroup(copy, grp[("fc", u)], a, b, raw[("fc", e)], H * half + 512 * g + a - 512 * half)
 
         def w_alloc(u):
             grp[("fc", u)] = grpp.tile([P, 1024, 4], BF16, name="grp_fc", align_bytes=64)
@@ -90,20 +107,15 @@ def tile_mlp_kernel(tc, x, c_fc, c_proj, gamma, mult_bias, out):
 
         def w_copy_s(u):
             vfc, vpj = SHARE.get(u, SHARE_DEFAULT)
-            if vfc < 1024:
-                regroup(nc.scalar.copy, grp[("fc", u)], raw[("fc", u)], vfc, 1024)
+            fc_copy(nc.scalar.copy, u, vfc, 1024)
             if vpj < 512:
-                regroup(nc.scalar.copy, grp[("pj", u)], raw[("pj", u)], vpj, 512)
+                regroup(nc.scalar.copy, grp[("pj", u)], vpj, 512, raw[("pj", u)], vpj)
 
         def w_copy_v(u):
             vfc, vpj = SHARE.get(u, SHARE_DEFAULT)
-            if vfc > 512:
-                regroup(nc.vector.tensor_copy, grp[("fc", u)], raw[("fc", u)], 0, 512)
-                regroup(nc.vector.tensor_copy, grp[("fc", u)], raw[("fc", u)], 512, vfc)
-            elif vfc > 0:
-                regroup(nc.vector.tensor_copy, grp[("fc", u)], raw[("fc", u)], 0, vfc)
+            fc_copy(nc.vector.tensor_copy, u, 0, vfc)
             if vpj > 0:
-                regroup(nc.vector.tensor_copy, grp[("pj", u)], raw[("pj", u)], 0, vpj)
+                regroup(nc.vector.tensor_copy, grp[("pj", u)], 0, vpj, raw[("pj", u)], 0)
 
         def w_copy(u):
             w_alloc(u)
@@ -244,12 +256,14 @@ def tile_mlp_kernel(tc, x, c_fc, c_proj, gamma, mult_bias, out):
 
         x_sb = const.tile([P, 8, D], BF16, name="x_sb")
         nc.sync.dma_start(out=x_sb[:, 0:4, :], in_=x[0].rearrange("e n d -> n e d"))
+        raw[("fc", 0)] = rawf.tile([P, 4, 2 * H], BF16, name="raw_fc")
         load_fc(0, 0)
         load_fc(0, 1)
         nc.sync.dma_start(out=x_sb[:, 4:8, :], in_=x[1].rearrange("e n d -> n e d"))
         load_pj(0)
         for u in range(1, RAW_BUFS):
             load(u)
+        load_fc_rows(1)
 
         ss = const.tile([P, 8], F32, name="ss")
         junk = const.tile([P, D], BF16, name="junk")
@@ -270,7 +284,7 @@ def tile_mlp_kernel(tc, x, c_fc, c_proj, gamma, mult_bias, out):
         warm3 = const.tile([P, 1], F32, name="warm3")
         nc.scalar.activation(out=warm3, in_=warm, func=ACT.Gelu)
         w_copy_s(0)
-        load(RAW_BUFS)
+        refill(0)
 
         gps = ps.tile([P, D], F32, tag="u", name="gps")
         nc.tensor.matmul(out=gps, lhsT=ones, rhs=g_row, start=True, stop=True)
@@ -307,7 +321,7 @@ def tile_mlp_kernel(tc, x, c_fc, c_proj, gamma, mult_bias, out):
         w_quant(0, "pj")
         mm1(0)
         w_copy(1)
-        load(RAW_BUFS + 1)
+        refill(1)
         h_quant(1)
 
         for k in range(UNITS):
@@ -330,7 +344,7 @@ def tile_mlp_kernel(tc, x, c_fc, c_proj, gamma, mult_bias, out):
                 mm2(k - 1)
             if k + 2 < UNITS:
                 w_copy(k + 2)
-                load(k + 2 + RAW_BUFS)
+                refill(k + 2)
             if k >= 1 and (k - 1) % 4 == 3:
                 store((k - 1) // 4, (nc.scalar.copy, nc.scalar.copy))
         g_regroup(UNITS - 1)

@@ -21,27 +21,18 @@ UNITS = NE * 4
 
 FLOPS = 2 * NE * TOK * (D * 2 * H + H * D)
 
-MANUAL = True
 RAW_BUFS = 4
-SHARE_DEFAULT = (304, 512)
-SHARE = {0: (1024, 0), 1: (512, 512)}
-
-
-def regroup(copy, dst, c0, c1, src, s0):
-    copy(
-        out=dst[:, c0:c1, :].rearrange("p (c i) t -> p c t i", i=4),
-        in_=src[:, :, s0 : s0 + c1 - c0].rearrange("p t (c i) -> p c t i", i=4),
-    )
+VFC = 160
+GPJ = 128
+SQ_COL = {0: 0, 1: 1, 4: 2, 5: 3, 2: 8, 3: 9, 6: 10, 7: 11}
 
 
 def tile_mlp_kernel(tc, x, c_fc, c_proj, gamma, mult_bias, out):
     nc = tc.nc
     with ExitStack() as ctx:
-        if MANUAL:
-            ctx.enter_context(tc.manual_schedule())
+        ctx.enter_context(tc.manual_schedule())
         const = ctx.enter_context(tc.tile_pool(name="const", bufs=1))
         rawp = ctx.enter_context(tc.tile_pool(name="raw", bufs=RAW_BUFS))
-        rawf = ctx.enter_context(tc.tile_pool(name="rawf", bufs=2))
         grpp = ctx.enter_context(tc.tile_pool(name="grp", bufs=3))
         codp = ctx.enter_context(tc.tile_pool(name="cod", bufs=4))
         actp = ctx.enter_context(tc.tile_pool(name="act", bufs=4))
@@ -63,16 +54,13 @@ def tile_mlp_kernel(tc, x, c_fc, c_proj, gamma, mult_bias, out):
 
         def load_fc(u, half):
             e, g = divmod(u, 4)
+            if half == 0:
+                raw[("fc", u)] = rawp.tile([P, 4, 1024], BF16, name="raw_fc")
             col = half * H + 512 * g
             nc.sync.dma_start(
-                out=raw[("fc", e)][:, :, col : col + 512],
+                out=raw[("fc", u)][:, :, 512 * half : 512 * half + 512],
                 in_=c_fc[e].rearrange("(t p) n -> p t n", p=P)[:, :, col : col + 512],
             )
-
-        def load_fc_rows(e):
-            raw[("fc", e)] = rawf.tile([P, 4, 2 * H], BF16, name="raw_fc")
-            for t in range(4):
-                nc.sync.dma_start(out=raw[("fc", e)][:, t, :], in_=c_fc[e, P * t : P * t + P, :])
 
         def load_pj(u):
             e, g = divmod(u, 4)
@@ -83,44 +71,28 @@ def tile_mlp_kernel(tc, x, c_fc, c_proj, gamma, mult_bias, out):
             )
 
         def load(u):
-            load_fc(u, 0)
-            load_fc(u, 1)
-            load_pj(u)
+            if u < UNITS:
+                load_fc(u, 0)
+                load_fc(u, 1)
+                load_pj(u)
 
-        def refill(u):
-            if u + RAW_BUFS < UNITS:
-                load_pj(u + RAW_BUFS)
-            if u % 4 == 3 and u // 4 + 2 < NE:
-                load_fc_rows(u // 4 + 2)
+        def w_alloc(u, which):
+            if which == "fc":
+                grp[("fc", u)] = grpp.tile([P, 1024, 4], BF16, name="grp_fc", align_bytes=64)
+            else:
+                grp[("pj", u)] = grpp.tile([P, 512, 4], BF16, name="grp_pj", bufs=1, align_bytes=64)
 
-        def fc_copy(copy, u, c0, c1):
-            e, g = divmod(u, 4)
-            for half in range(2):
-                a = max(c0, 512 * half)
-                b = min(c1, 512 * half + 512)
-                if a < b:
-                    regroup(copy, grp[("fc", u)], a, b, raw[("fc", e)], H * half + 512 * g + a - 512 * half)
-
-        def w_alloc(u):
-            grp[("fc", u)] = grpp.tile([P, 1024, 4], BF16, name="grp_fc", align_bytes=64)
-            grp[("pj", u)] = grpp.tile([P, 512, 4], BF16, name="grp_pj", align_bytes=64)
-
-        def w_copy_s(u):
-            vfc, vpj = SHARE.get(u, SHARE_DEFAULT)
-            fc_copy(nc.scalar.copy, u, vfc, 1024)
-            if vpj < 512:
-                regroup(nc.scalar.copy, grp[("pj", u)], vpj, 512, raw[("pj", u)], vpj)
-
-        def w_copy_v(u):
-            vfc, vpj = SHARE.get(u, SHARE_DEFAULT)
-            fc_copy(nc.vector.tensor_copy, u, 0, vfc)
-            if vpj > 0:
-                regroup(nc.vector.tensor_copy, grp[("pj", u)], 0, vpj, raw[("pj", u)], 0)
-
-        def w_copy(u):
-            w_alloc(u)
-            w_copy_s(u)
-            w_copy_v(u)
+        def piece(eng, u, which, c0, c1):
+            dst = grp[(which, u)][:, c0:c1, :].rearrange("p (c i) t -> p c t i", i=4)
+            src = raw[(which, u)][:, :, c0:c1].rearrange("p t (c i) -> p c t i", i=4)
+            if eng == "V":
+                nc.vector.tensor_copy(out=dst, in_=src)
+            elif eng == "S":
+                nc.scalar.copy(out=dst, in_=src)
+            else:
+                nc.gpsimd.tensor_scalar(
+                    out=dst, in0=src, scalar1=1.0, scalar2=0.0, op0=ALU.mult, op1=ALU.add
+                )
 
         def w_quant(u, which):
             width = 1024 if which == "fc" else 512
@@ -161,14 +133,14 @@ def tile_mlp_kernel(tc, x, c_fc, c_proj, gamma, mult_bias, out):
 
         def g_mul(u):
             g = u % 4
-            planes = gp.tile([P, TOK // 8, 4, 8], BF16, name="planes")
+            planes = gp.tile([P, 4, TOK], BF16, name="planes")
             pla[u] = planes
             for c in range(4):
                 nc.vector.scalar_tensor_tensor(
-                    out=planes[:, :, c, :],
-                    in0=bank[("v", u, c // 2)][:, c % 2, :].rearrange("p (a b) -> p a b", b=8),
+                    out=planes[:, c, :],
+                    in0=bank[("v", u, c // 2)][:, c % 2, :],
                     scalar=mbT[:, 4 * g + c : 4 * g + c + 1],
-                    in1=gel[(u, c // 2)][:, c % 2, :].rearrange("p (a b) -> p a b", b=8),
+                    in1=gel[(u, c // 2)][:, c % 2, :],
                     op0=ALU.mult,
                     op1=ALU.mult,
                 )
@@ -177,26 +149,9 @@ def tile_mlp_kernel(tc, x, c_fc, c_proj, gamma, mult_bias, out):
             gg = gp.tile([P, TOK, 4], BF16, name="gg", align_bytes=64)
             grp[("g", u)] = gg
             nc.vector.tensor_copy(
-                out=gg.rearrange("p (a b) t -> p a b t", b=8),
-                in_=pla[u].rearrange("p a t b -> p a b t"),
+                out=gg.rearrange("p (c i) t -> p c t i", i=4),
+                in_=pla[u].rearrange("p t (c i) -> p c t i", i=4),
             )
-
-        def g_inter(u):
-            pb = ps.tile([P, TOK, 4], BF16, tag="u", name="pb")
-            bank[("b", u)] = pb
-            for j in range(NB):
-                nc.tensor.matmul(
-                    out=pb[:, P * j : P * j + P, :].rearrange("p r t -> p (r t)"),
-                    lhsT=ident,
-                    rhs=pla[u][:, 16 * j : 16 * j + 16, :, :].rearrange("p a t b -> p a b t"),
-                    start=True,
-                    stop=True,
-                )
-
-        def g_copy(u):
-            gg = gp.tile([P, TOK, 4], BF16, name="gg", align_bytes=64)
-            grp[("g", u)] = gg
-            nc.scalar.copy(out=gg, in_=bank[("b", u)])
 
         def g_quant(u):
             codes = gp.tile([P, TOK], U32, name="gq_c", align_bytes=64)
@@ -232,6 +187,29 @@ def tile_mlp_kernel(tc, x, c_fc, c_proj, gamma, mult_bias, out):
                 copies[b](out=osb, in_=acc[(e, b)])
                 nc.sync.dma_start(out=out[b, e], in_=osb)
 
+        def h_mul(e):
+            for b in range(NB):
+                i = 4 * b + e
+                nc.vector.scalar_tensor_tensor(
+                    out=h_sb[:, i, :],
+                    in0=x_sb[:, i, :],
+                    scalar=rn[:, SQ_COL[i] : SQ_COL[i] + 1],
+                    in1=gps,
+                    op0=ALU.mult,
+                    op1=ALU.mult,
+                )
+            pT = ps.tile([P, NB, 4, P], BF16, tag="u", name="pT")
+            bank[("T", e)] = pT
+            for b in range(NB):
+                for t in range(4):
+                    nc.tensor.transpose(
+                        pT[:, b, t, :], h_sb[:, 4 * b + e, P * t : P * t + P], ident
+                    )
+
+        def h_copy(e):
+            hgs[e] = hgp.tile([P, NB, P, 4], BF16, name="hg", align_bytes=64)
+            nc.scalar.copy(out=hgs[e], in_=bank[("T", e)].rearrange("p b t r -> p b r t"))
+
         def h_quant(e):
             nc.vector.quantize_mx(
                 out=hq_c[:, e, :].bitcast(FP8X4),
@@ -249,42 +227,54 @@ def tile_mlp_kernel(tc, x, c_fc, c_proj, gamma, mult_bias, out):
         nc.vector.memset(ones, 1.0)
         warm = const.tile([P, 1], F32, name="warm")
         nc.vector.memset(warm, 1.0)
+        ss = const.tile([P, 16], F32, name="ss")
+        nc.vector.memset(ss, 1.0)
         warm2 = const.tile([P, 1], F32, name="warm2")
         nc.scalar.activation(out=warm2, in_=warm, func=ACT.Sqrt)
         ident = const.tile([P, P], BF16, name="ident")
         make_identity(nc, ident)
 
         x_sb = const.tile([P, 8, D], BF16, name="x_sb")
-        nc.sync.dma_start(out=x_sb[:, 0:4, :], in_=x[0].rearrange("e n d -> n e d"))
-        raw[("fc", 0)] = rawf.tile([P, 4, 2 * H], BF16, name="raw_fc")
-        load_fc(0, 0)
-        load_fc(0, 1)
-        nc.sync.dma_start(out=x_sb[:, 4:8, :], in_=x[1].rearrange("e n d -> n e d"))
-        load_pj(0)
-        for u in range(1, RAW_BUFS):
+        for b in range(NB):
+            for hf in range(2):
+                i0 = 4 * b + 2 * hf
+                nc.sync.dma_start(
+                    out=x_sb[:, i0 : i0 + 2, :],
+                    in_=x[b, 2 * hf : 2 * hf + 2].rearrange("e n d -> n e d"),
+                )
+        for u in range(RAW_BUFS):
             load(u)
-        load_fc_rows(1)
 
-        ss = const.tile([P, 8], F32, name="ss")
-        junk = const.tile([P, D], BF16, name="junk")
-        for i in range(8):
-            nc.scalar.activation(
-                out=junk, in_=x_sb[:, i, :], func=ACT.Square, accum_out=ss[:, i : i + 1]
-            )
-        w_alloc(0)
-        w_copy_v(0)
-        ssc = const.tile([P, 8], F32, name="ssc")
+        junk_s = const.tile([P, D], BF16, name="junk_s")
+        junk_v = const.tile([P, D], F32, name="junk_v")
+        for b in range(NB):
+            for i in (4 * b, 4 * b + 1):
+                nc.scalar.activation(
+                    out=junk_s,
+                    in_=x_sb[:, i, :],
+                    func=ACT.Square,
+                    accum_out=ss[:, SQ_COL[i] : SQ_COL[i] + 1],
+                )
+            for i in (4 * b + 2, 4 * b + 3):
+                nc.vector.scalar_tensor_tensor(
+                    out=junk_v,
+                    in0=x_sb[:, i, :],
+                    scalar=1.0,
+                    in1=x_sb[:, i, :],
+                    op0=ALU.mult,
+                    op1=ALU.mult,
+                    accum_out=ss[:, SQ_COL[i] : SQ_COL[i] + 1],
+                )
+        ssc = const.tile([P, 16], F32, name="ssc")
         nc.vector.tensor_scalar(
             out=ssc, in0=ss, scalar1=1e-24, scalar2=1.0 / D, op0=ALU.max, op1=ALU.mult
         )
-        l2 = const.tile([P, 8], F32, name="l2")
+        l2 = const.tile([P, 16], F32, name="l2")
         nc.scalar.activation(out=l2, in_=ssc, func=ACT.Sqrt)
-        rn = const.tile([P, 8], F32, name="rn")
+        rn = const.tile([P, 16], F32, name="rn")
         nc.vector.reciprocal(out=rn, in_=l2)
         warm3 = const.tile([P, 1], F32, name="warm3")
         nc.scalar.activation(out=warm3, in_=warm, func=ACT.Gelu)
-        w_copy_s(0)
-        refill(0)
 
         gps = ps.tile([P, D], F32, tag="u", name="gps")
         nc.tensor.matmul(out=gps, lhsT=ones, rhs=g_row, start=True, stop=True)
@@ -296,58 +286,60 @@ def tile_mlp_kernel(tc, x, c_fc, c_proj, gamma, mult_bias, out):
         h_sb = const.tile([P, 8, D], BF16, name="h_sb")
         hq_c = const.tile([P, NE, TOK], U32, name="hq_c", align_bytes=64)
         hq_s = const.tile([P, NE, TOK], U8, name="hq_s", align_bytes=64)
-        for e in range(NE):
-            for b in range(NB):
-                i = 4 * b + e
-                nc.vector.scalar_tensor_tensor(
-                    out=h_sb[:, i, :],
-                    in0=x_sb[:, i, :],
-                    scalar=rn[:, i : i + 1],
-                    in1=gps,
-                    op0=ALU.mult,
-                    op1=ALU.mult,
-                )
-            pT = ps.tile([P, NB, 4, P], BF16, tag="u", name="pT")
-            for b in range(NB):
-                for t in range(4):
-                    nc.tensor.transpose(
-                        pT[:, b, t, :], h_sb[:, 4 * b + e, P * t : P * t + P], ident
-                    )
-            hgs[e] = hgp.tile([P, NB, P, 4], BF16, name="hg", align_bytes=64)
-            nc.scalar.copy(out=hgs[e], in_=pT.rearrange("p b t r -> p b r t"))
 
+        w_alloc(0, "fc")
+        w_alloc(0, "pj")
+        h_mul(0)
+        h_mul(1)
+        piece("S", 0, "fc", 0, 512)
+        piece("V", 0, "fc", 512, 1024)
+        h_copy(0)
+        h_mul(2)
+        h_mul(3)
+        piece("S", 0, "pj", 0, 512)
+        load(RAW_BUFS)
         w_quant(0, "fc")
         h_quant(0)
-        w_quant(0, "pj")
+        h_copy(1)
         mm1(0)
-        w_copy(1)
-        refill(1)
+        w_alloc(1, "fc")
+        piece("V", 1, "fc", 0, 512)
+        piece("S", 1, "fc", 512, 1024)
+        w_quant(0, "pj")
+        w_alloc(1, "pj")
+        piece("V", 1, "pj", 0, 512)
+        load(RAW_BUFS + 1)
         h_quant(1)
+        h_copy(2)
+        h_copy(3)
 
         for k in range(UNITS):
             if k + 1 < UNITS:
                 w_quant(k + 1, "fc")
+            if k >= 1:
+                g_quant(k - 1)
             if k < 2:
                 h_quant(k + 2)
             if k + 1 < UNITS:
                 w_quant(k + 1, "pj")
-            g_gelu(k)
+            if k + 2 < UNITS:
+                w_alloc(k + 2, "pj")
+                piece("G", k + 2, "pj", 512 - GPJ, 512)
             if k >= 1:
-                g_copy(k - 1)
+                mm2(k - 1)
+            g_gelu(k)
             if k + 1 < UNITS:
                 mm1(k + 1)
             g_mul(k)
-            if k + 1 < UNITS:
-                g_inter(k)
-            if k >= 1:
-                g_quant(k - 1)
-                mm2(k - 1)
             if k + 2 < UNITS:
-                w_copy(k + 2)
-                refill(k + 2)
+                w_alloc(k + 2, "fc")
+                piece("S", k + 2, "fc", VFC, 1024)
+                piece("V", k + 2, "fc", 0, VFC)
+                piece("V", k + 2, "pj", 0, 512 - GPJ)
+                load(k + 2 + RAW_BUFS)
             if k >= 1 and (k - 1) % 4 == 3:
                 store((k - 1) // 4, (nc.scalar.copy, nc.scalar.copy))
-        g_regroup(UNITS - 1)
+            g_regroup(k)
         g_quant(UNITS - 1)
         mm2(UNITS - 1)
         store(NE - 1, (nc.scalar.copy, nc.vector.tensor_copy))

@@ -23,7 +23,7 @@ FLOPS = 2 * NE * TOK * (D * 2 * H + H * D)
 
 RAW_BUFS = 4
 VFC = 160
-GPJ = 128
+GPJ = 192
 SQ_COL = {0: 0, 1: 1, 4: 2, 5: 3, 2: 8, 3: 9, 6: 10, 7: 11}
 
 
@@ -316,8 +316,6 @@ def tile_mlp_kernel(tc, x, c_fc, c_proj, gamma, mult_bias, out):
         for k in range(UNITS):
             if k + 1 < UNITS:
                 w_quant(k + 1, "fc")
-            if k >= 1:
-                g_quant(k - 1)
             if k < 2:
                 h_quant(k + 2)
             if k + 1 < UNITS:
@@ -326,6 +324,7 @@ def tile_mlp_kernel(tc, x, c_fc, c_proj, gamma, mult_bias, out):
                 w_alloc(k + 2, "pj")
                 piece("G", k + 2, "pj", 512 - GPJ, 512)
             if k >= 1:
+                g_quant(k - 1)
                 mm2(k - 1)
             g_gelu(k)
             if k + 1 < UNITS:

@@ -22,7 +22,7 @@ UNITS = NE * 4
 FLOPS = 2 * NE * TOK * (D * 2 * H + H * D)
 
 RAW_BUFS = 4
-VFC = 160
+VFC = 184
 GPJ = 192
 SQ_COL = {0: 0, 1: 1, 4: 2, 5: 3, 2: 8, 3: 9, 6: 10, 7: 11}
 
@@ -316,6 +316,8 @@ def tile_mlp_kernel(tc, x, c_fc, c_proj, gamma, mult_bias, out):
         for k in range(UNITS):
             if k + 1 < UNITS:
                 w_quant(k + 1, "fc")
+            if k >= 1:
+                g_quant(k - 1)
             if k < 2:
                 h_quant(k + 2)
             if k + 1 < UNITS:
@@ -324,7 +326,6 @@ def tile_mlp_kernel(tc, x, c_fc, c_proj, gamma, mult_bias, out):
                 w_alloc(k + 2, "pj")
                 piece("G", k + 2, "pj", 512 - GPJ, 512)
             if k >= 1:
-                g_quant(k - 1)
                 mm2(k - 1)
             g_gelu(k)
             if k + 1 < UNITS:

from contextlib import ExitStack

import concourse.mybir as mybir
from concourse.masks import make_identity

BF16 = mybir.dt.bfloat16
F32 = mybir.dt.float32
U32 = mybir.dt.uint32
U8 = mybir.dt.uint8
FP8X4 = mybir.dt.float8_e4m3fn_x4
ACT = mybir.ActivationFunctionType
ALU = mybir.AluOpType

P = 128
D = 512
H = 2048
NE = 4
NB = 2
TOK = NB * P
UNITS = NE * 4

FLOPS = 2 * NE * TOK * (D * 2 * H + H * D)

RAW_BUFS = 4
VFC = 184
GPJ = 192
SQ_COL = {0: 0, 1: 1, 4: 2, 5: 3, 2: 8, 3: 9, 6: 10, 7: 11}


def tile_mlp_kernel(tc, x, c_fc, c_proj, gamma, mult_bias, out):
    nc = tc.nc
    with ExitStack() as ctx:
        ctx.enter_context(tc.manual_schedule())
        const = ctx.enter_context(tc.tile_pool(name="const", bufs=1))
        rawp = ctx.enter_context(tc.tile_pool(name="raw", bufs=RAW_BUFS))
        grpp = ctx.enter_context(tc.tile_pool(name="grp", bufs=3))
        codp = ctx.enter_context(tc.tile_pool(name="cod", bufs=4))
        actp = ctx.enter_context(tc.tile_pool(name="act", bufs=4))
        gp = ctx.enter_context(tc.tile_pool(name="g", bufs=2))
        outp = ctx.enter_context(tc.tile_pool(name="outp", bufs=4))
        hgp = ctx.enter_context(tc.tile_pool(name="hgp", bufs=4))
        ps = ctx.enter_context(tc.psum_pool(name="ps", bufs=6))
        pso = ctx.enter_context(tc.psum_pool(name="pso", bufs=1))

        raw = {}
        cod = {}
        grp = {}
        bank = {}
        gel = {}
        pla = {}
        gq = {}
        acc = {}
        hgs = {}

        def load_fc(u, half):
            e, g = divmod(u, 4)
            if half == 0:
                raw[("fc", u)] = rawp.tile([P, 4, 1024], BF16, name="raw_fc")
            col = half * H + 512 * g
            nc.sync.dma_start(
                out=raw[("fc", u)][:, :, 512 * half : 512 * half + 512],
                in_=c_fc[e].rearrange("(t p) n -> p t n", p=P)[:, :, col : col + 512],
            )

        def load_pj(u):
            e, g = divmod(u, 4)
            raw[("pj", u)] = rawp.tile([P, 4, 512], BF16, name="raw_pj")
            nc.sync.dma_start(
                out=raw[("pj", u)],
                in_=c_proj[e, 512 * g : 512 * g + 512, :].rearrange("(t p) n -> p t n", p=P),
            )

        def load(u):
            if u < UNITS:
                load_fc(u, 0)
                load_fc(u, 1)
                load_pj(u)

        def w_alloc(u, which):
            if which == "fc":
                grp[("fc", u)] = grpp.tile([P, 1024, 4], BF16, name="grp_fc", align_bytes=64)
            else:
                grp[("pj", u)] = grpp.tile([P, 512, 4], BF16, name="grp_pj", bufs=1, align_bytes=64)

        def piece(eng, u, which, c0, c1):
            dst = grp[(which, u)][:, c0:c1, :].rearrange("p (c i) t -> p c t i", i=4)
            src = raw[(which, u)][:, :, c0:c1].rearrange("p t (c i) -> p c t i", i=4)
            if eng == "V":
                nc.vector.tensor_copy(out=dst, in_=src)
            elif eng == "S":
                nc.scalar.copy(out=dst, in_=src)
            else:
                nc.gpsimd.tensor_scalar(
                    out=dst, in0=src, scalar1=1.0, scalar2=0.0, op0=ALU.mult, op1=ALU.add
                )

        def w_quant(u, which):
            width = 1024 if which == "fc" else 512
            codes = codp.tile([P, width], U32, name="cod_" + which, align_bytes=64)
            scales = codp.tile([P, width], U8, name="scl_" + which, align_bytes=64)
            cod[(which, u)] = (codes, scales)
            nc.vector.quantize_mx(
                out=codes.bitcast(FP8X4),
                scales=scales,
                in_=grp[(which, u)].rearrange("p w j -> p (w j)"),
            )

        def mm1(u):
            e = u // 4
            codes, scales = cod[("fc", u)]
            for kind in ("g", "v"):
                base = 512 if kind == "g" else 0
                for j in range(2):
                    pt = ps.tile([P, 2, TOK], F32, tag="u", name="p" + kind)
                    bank[(kind, u, j)] = pt
                    for s in range(2):
                        c0 = base + 128 * (2 * j + s)
                        nc.tensor.matmul_mx(
                            out=pt[:, s, :],
                            lhsT=codes[:, c0 : c0 + 128].bitcast(FP8X4),
                            lhsT_scale=scales[:, c0 : c0 + 128],
                            rhs=hq_c[:, e, :].bitcast(FP8X4),
                            rhs_scale=hq_s[:, e, :],
                            start=True,
                            stop=True,
                        )

        def g_gelu(u):
            for j in range(2):
                a = actp.tile([P, 2, TOK], F32, name="gelu")
                gel[(u, j)] = a
                nc.scalar.activation(out=a, in_=bank[("g", u, j)], func=ACT.Gelu)

        def g_mul(u):
            g = u % 4
            planes = gp.tile([P, 4, TOK], BF16, name="planes")
            pla[u] = planes
            for c in range(4):
                nc.vector.scalar_tensor_tensor(
                    out=planes[:, c, :],
                    in0=bank[("v", u, c // 2)][:, c % 2, :],
                    scalar=mbT[:, 4 * g + c : 4 * g + c + 1],
                    in1=gel[(u, c // 2)][:, c % 2, :],
                    op0=ALU.mult,
                    op1=ALU.mult,
                )

        def g_regroup(u):
            gg = gp.tile([P, TOK, 4], BF16, name="gg", align_bytes=64)
            grp[("g", u)] = gg
            nc.vector.tensor_copy(
                out=gg.rearrange("p (c i) t -> p c t i", i=4),
                in_=pla[u].rearrange("p t (c i) -> p c t i", i=4),
            )

        def g_quant(u):
            codes = gp.tile([P, TOK], U32, name="gq_c", align_bytes=64)
            scales = gp.tile([P, TOK], U8, name="gq_s", align_bytes=64)
            gq[u] = (codes, scales)
            nc.vector.quantize_mx(
                out=codes.bitcast(FP8X4),
                scales=scales,
                in_=grp[("g", u)].rearrange("p w j -> p (w j)"),
            )

        def mm2(u):
            e, g = divmod(u, 4)
            if g == 0:
                for b in range(NB):
                    acc[(e, b)] = pso.tile([P, D], F32, tag="po%d" % b, name="po%d" % b)
            codes, scales = gq[u]
            wc, ws = cod[("pj", u)]
            for b in range(NB):
                nc.tensor.matmul_mx(
                    out=acc[(e, b)],
                    lhsT=codes[:, P * b : P * b + P].bitcast(FP8X4),
                    lhsT_scale=scales[:, P * b : P * b + P],
                    rhs=wc.bitcast(FP8X4),
                    rhs_scale=ws,
                    start=(g == 0),
                    stop=(g == 3),
                )

        def store(e, copies):
            for b in range(NB):
                osb = outp.tile([P, D], F32, name="osb")
                copies[b](out=osb, in_=acc[(e, b)])
                nc.sync.dma_start(out=out[b, e], in_=osb)

        def h_mul(e):
            for b in range(NB):
                i = 4 * b + e
                nc.vector.scalar_tensor_tensor(
                    out=h_sb[:, i, :],
                    in0=x_sb[:, i, :],
                    scalar=rn[:, SQ_COL[i] : SQ_COL[i] + 1],
                    in1=gps,
                    op0=ALU.mult,
                    op1=ALU.mult,
                )
            pT = ps.tile([P, NB, 4, P], BF16, tag="u", name="pT")
            bank[("T", e)] = pT
            for b in range(NB):
                for t in range(4):
                    nc.tensor.transpose(
                        pT[:, b, t, :], h_sb[:, 4 * b + e, P * t : P * t + P], ident
                    )

        def h_copy(e):
            hgs[e] = hgp.tile([P, NB, P, 4], BF16, name="hg", align_bytes=64)
            nc.scalar.copy(out=hgs[e], in_=bank[("T", e)].rearrange("p b t r -> p b r t"))

        def h_quant(e):
            nc.vector.quantize_mx(
                out=hq_c[:, e, :].bitcast(FP8X4),
                scales=hq_s[:, e, :],
                in_=hgs[e].rearrange("p b r t -> p (b r t)"),
            )

        g_row = const.tile([P, D], BF16, name="g_row")
        nc.vector.memset(g_row, 0.0)
        nc.scalar.dma_start(out=g_row[0:1, :], in_=gamma.rearrange("(o d) -> o d", o=1))
        mb_rows = const.tile([P, P], BF16, name="mb_rows")
        nc.vector.memset(mb_rows, 0.0)
        nc.scalar.dma_start(out=mb_rows[0:16, :], in_=mult_bias.rearrange("(c p) -> c p", p=P))
        ones = const.tile([P, P], BF16, name="ones")
        nc.vector.memset(ones, 1.0)
        warm = const.tile([P, 1], F32, name="warm")
        nc.vector.memset(warm, 1.0)
        ss = const.tile([P, 16], F32, name="ss")
        nc.vector.memset(ss, 1.0)
        warm2 = const.tile([P, 1], F32, name="warm2")
        nc.scalar.activation(out=warm2, in_=warm, func=ACT.Sqrt)
        ident = const.tile([P, P], BF16, name="ident")
        make_identity(nc, ident)

        x_sb = const.tile([P, 8, D], BF16, name="x_sb")
        for b in range(NB):
            for hf in range(2):
                i0 = 4 * b + 2 * hf
                nc.sync.dma_start(
                    out=x_sb[:, i0 : i0 + 2, :],
                    in_=x[b, 2 * hf : 2 * hf + 2].rearrange("e n d -> n e d"),
                )
        for u in range(RAW_BUFS):
            load(u)

        junk_s = const.tile([P, D], BF16, name="junk_s")
        junk_v = const.tile([P, D], F32, name="junk_v")
        for b in range(NB):
            for i in (4 * b, 4 * b + 1):
                nc.scalar.activation(
                    out=junk_s,
                    in_=x_sb[:, i, :],
                    func=ACT.Square,
                    accum_out=ss[:, SQ_COL[i] : SQ_COL[i] + 1],
                )
            for i in (4 * b + 2, 4 * b + 3):
                nc.vector.scalar_tensor_tensor(
                    out=junk_v,
                    in0=x_sb[:, i, :],
                    scalar=1.0,
                    in1=x_sb[:, i, :],
                    op0=ALU.mult,
                    op1=ALU.mult,
                    accum_out=ss[:, SQ_COL[i] : SQ_COL[i] + 1],
                )
        ssc = const.tile([P, 16], F32, name="ssc")
        nc.vector.tensor_scalar(
            out=ssc, in0=ss, scalar1=1e-24, scalar2=1.0 / D, op0=ALU.max, op1=ALU.mult
        )
        l2 = const.tile([P, 16], F32, name="l2")
        nc.scalar.activation(out=l2, in_=ssc, func=ACT.Sqrt)
        rn = const.tile([P, 16], F32, name="rn")
        nc.vector.reciprocal(out=rn, in_=l2)
        warm3 = const.tile([P, 1], F32, name="warm3")
        nc.scalar.activation(out=warm3, in_=warm, func=ACT.Gelu)

        gps = ps.tile([P, D], F32, tag="u", name="gps")
        nc.tensor.matmul(out=gps, lhsT=ones, rhs=g_row, start=True, stop=True)
        pm = ps.tile([P, P], BF16, tag="u", name="pm")
        nc.tensor.transpose(pm, mb_rows, ident)
        mbT = const.tile([P, 16], F32, name="mbT")
        nc.vector.tensor_copy(out=mbT, in_=pm[:, 0:16])

        h_sb = const.tile([P, 8, D], BF16, name="h_sb")
        hq_c = const.tile([P, NE, TOK], U32, name="hq_c", align_bytes=64)
        hq_s = const.tile([P, NE, TOK], U8, name="hq_s", align_bytes=64)

        w_alloc(0, "fc")
        w_alloc(0, "pj")
        h_mul(0)
        h_mul(1)
        piece("S", 0, "fc", 0, 512)
        piece("V", 0, "fc", 512, 1024)
        h_copy(0)
        h_mul(2)
        h_mul(3)
        piece("S", 0, "pj", 0, 512)
        load(RAW_BUFS)
        w_quant(0, "fc")
        h_quant(0)
        h_copy(1)
        mm1(0)
        w_alloc(1, "fc")
        piece("V", 1, "fc", 0, 512)
        piece("S", 1, "fc", 512, 1024)
        w_quant(0, "pj")
        w_alloc(1, "pj")
        piece("V", 1, "pj", 0, 512)
        load(RAW_BUFS + 1)
        h_quant(1)
        h_copy(2)
        h_copy(3)

        for k in range(UNITS):
            if k + 1 < UNITS:
                w_quant(k + 1, "fc")
            if k >= 1:
                g_quant(k - 1)
            if k < 2:
                h_quant(k + 2)
            if k + 1 < UNITS:
                w_quant(k + 1, "pj")
            if k + 2 < UNITS:
                w_alloc(k + 2, "pj")
                piece("G", k + 2, "pj", 512 - GPJ, 512)
            if k >= 1:
                mm2(k - 1)
            g_gelu(k)
            if k + 1 < UNITS:
                mm1(k + 1)
            g_mul(k)
            if k + 2 < UNITS:
                w_alloc(k + 2, "fc")
                piece("S", k + 2, "fc", VFC, 1024)
                piece("V", k + 2, "fc", 0, VFC)
                piece("V", k + 2, "pj", 0, 512 - GPJ)
                load(k + 2 + RAW_BUFS)
            if k >= 1 and (k - 1) % 4 == 3:
                store((k - 1) // 4, (nc.scalar.copy, nc.scalar.copy))
            g_regroup(k)
        g_quant(UNITS - 1)
        mm2(UNITS - 1)
        store(NE - 1, (nc.scalar.copy, nc.vector.tensor_copy))
